import numpy as np
import ml_dtypes


def mxq(x, axis, fmt="e4m3"):
    dtype, down = {"e4m3": (ml_dtypes.float8_e4m3fn, 7), "e5m2": (ml_dtypes.float8_e5m2, 14)}[fmt]
    v = np.moveaxis(np.asarray(x, np.float32).astype(ml_dtypes.bfloat16).astype(np.float64), axis, -1)
    blocks = v.reshape(v.shape[:-1] + (-1, 32))
    amax = np.abs(blocks).max(-1, keepdims=True)
    byte = np.maximum(np.where(amax > 0, np.frexp(amax)[1] - 1 + 127, 0) - down, 1)
    scale = np.exp2(byte - 127.0)
    codes = (blocks / scale).astype(np.float32).astype(dtype).astype(np.float64)
    return np.moveaxis((codes * scale).reshape(v.shape), -1, axis)


WIDE = False


def mx_kscale(k):
    if not WIDE:
        return np.ones(k)
    levels = np.array([10, -10, 5, -5, 0])
    a = np.random.permutation(np.resize(levels, k // 512 * 4)).reshape(k // 512, 4)
    idx = np.arange(k)
    return np.exp2(a[idx // 512, idx % 128 // 32])


BF16 = ml_dtypes.bfloat16


def bf(x):
    return np.asarray(x, np.float32).astype(BF16)


def f64(x):
    return np.asarray(x).astype(np.float64)


B, S, E, N_HEAD, MP_NUM, ROTARY_DIM = 2, 128, 2048, 16, 4, 64
HEAD_DIM = E // N_HEAD
LOCAL = E // MP_NUM
ROPE_BASE = 10000.0


def rotate_every_two(x):
    x1 = x[..., 0::2]
    x2 = x[..., 1::2]
    return np.stack((-x2, x1), axis=-1).reshape(x.shape)


def rope(x, sin, cos):
    x_rot = x[..., :ROTARY_DIM]
    x_pass = x[..., ROTARY_DIM:]
    x_rot = x_rot * cos + rotate_every_two(x_rot) * sin
    return np.concatenate([x_rot, x_pass], axis=-1)


def setup_inputs():
    s = mx_kscale(E)
    return {"hidden_states": bf(np.random.standard_normal((B, S, E)) * s),
            "w_qkv": bf(np.random.standard_normal((3 * E, E)) / np.sqrt(E) / s[None, :])}


def reference(hidden_states, w_qkv):
    qkv = mxq(f64(hidden_states), 2, "e4m3") @ mxq(f64(w_qkv), 1, "e4m3").T
    qkv = qkv.reshape(B, S, MP_NUM, 3 * LOCAL)
    q = qkv[..., :LOCAL].reshape(B, S, N_HEAD, HEAD_DIM)
    v = qkv[..., LOCAL:2 * LOCAL].reshape(B, S, N_HEAD, HEAD_DIM)
    k = qkv[..., 2 * LOCAL:].reshape(B, S, N_HEAD, HEAD_DIM)
    inv_freq = 1.0 / (ROPE_BASE ** (np.arange(0, ROTARY_DIM, 2) / ROTARY_DIM))
    freqs = np.arange(S)[:, None] * inv_freq[None, :]
    sin = np.repeat(np.sin(freqs), 2, axis=-1)[None, :, None, :]
    cos = np.repeat(np.cos(freqs), 2, axis=-1)[None, :, None, :]
    q = rope(q, sin, cos)
    k = rope(k, sin, cos)
    return q.transpose(0, 2, 1, 3), k.transpose(0, 2, 1, 3), v.transpose(0, 2, 1, 3)

@@ -1,0 +1,233 @@
+import math
+from contextlib import ExitStack
+
+import concourse.mybir as mybir
+from concourse.masks import make_identity
+
+F32 = mybir.dt.float32
+BF16 = mybir.dt.bfloat16
+I32 = mybir.dt.int32
+U32 = mybir.dt.uint32
+U8 = mybir.dt.uint8
+FP8X4 = mybir.dt.float8_e4m3fn_x4
+ALU = mybir.AluOpType
+ACT = mybir.ActivationFunctionType
+
+P = 128
+BATCH = 2
+E = 2048
+SHARDS = 4
+LOCAL = 512
+HEAD_DIM = 128
+PAIRS = 32
+ROPE_BASE = 10000.0
+
+PACK = 4
+K_PASS = P * PACK
+PASSES = E // K_PASS
+WORDS = K_PASS // 2
+
+BLOCK = 256
+BLOCK_HEADS = BLOCK // HEAD_DIM
+BLOCKS = 3 * SHARDS * LOCAL // BLOCK
+PREFETCH = 7
+
+FLOPS = 2 * BATCH * P * 3 * SHARDS * LOCAL * E
+
+ROUND_MAGIC = 12582912.0
+TWO_PI_HIGH = 6.28125
+TWO_PI_LOW = 2.0 * math.pi - TWO_PI_HIGH
+
+
+def tile_ttcodegenattention_pa_kernel(tc, hidden_states, w_qkv, out_0, out_1, out_2):
+    nc = tc.nc
+
+    blocks = []
+    for shard in range(SHARDS):
+        for part_row, dest, rotated in ((0, out_0, True), (2 * LOCAL, out_1, True), (LOCAL, out_2, False)):
+            for half in range(LOCAL // BLOCK):
+                blocks.append(
+                    (
+                        shard * 3 * LOCAL + part_row + half * BLOCK,
+                        dest,
+                        (shard * LOCAL + half * BLOCK) // HEAD_DIM,
+                        rotated,
+                    )
+                )
+
+    with ExitStack() as ctx:
+        ctx.enter_context(tc.manual_schedule())
+        consts = ctx.enter_context(tc.tile_pool(name="consts", bufs=1))
+        raw_pool = ctx.enter_context(tc.tile_pool(name="raw", bufs=PREFETCH + 1))
+        grouped_pool = ctx.enter_context(tc.tile_pool(name="grouped", bufs=3))
+        codes_pool = ctx.enter_context(tc.tile_pool(name="codes", bufs=3))
+        result_pool = ctx.enter_context(tc.tile_pool(name="result", bufs=4))
+        bank_pool = ctx.enter_context(tc.psum_pool(name="banks", bufs=6))
+        acc_pool = ctx.enter_context(tc.psum_pool(name="acc", bufs=2))
+
+        def load_weights(kb):
+            row = blocks[kb][0]
+            w_raw = raw_pool.tile([P, 2, E], BF16, name="w_raw")
+            nc.sync.dma_start(
+                out=w_raw[:], in_=w_qkv[row : row + BLOCK, :].rearrange("(j t) k -> j t k", t=2)
+            )
+            return w_raw
+
+        def transpose_and_group(word_views, grouped):
+            bank = bank_pool.tile([P, 2, 2, P], F32, name="bank")
+            for s in range(2):
+                for u in range(2):
+                    nc.tensor.transpose(bank[:, s, u, :], word_views[s][:, u * P : (u + 1) * P], ident[:])
+            nc.scalar.copy(
+                out=grouped.bitcast(F32).rearrange("p (s r u) -> p s r u", s=2, u=2),
+                in_=bank[:].rearrange("p s u r -> p s r u"),
+            )
+
+        def prepare_weights(w_raw):
+            w_grouped = grouped_pool.tile([P, PASSES, PACK * BLOCK], BF16, name="w_grouped", align_bytes=64)
+            w_codes = codes_pool.tile([P, PASSES, BLOCK], U32, name="w_codes", align_bytes=64)
+            w_scales = codes_pool.tile([P, PASSES, BLOCK], U8, name="w_scales", align_bytes=64)
+            for g in range(PASSES):
+                transpose_and_group(
+                    [w_raw[:, t, :].bitcast(F32)[:, g * WORDS : (g + 1) * WORDS] for t in range(2)],
+                    w_grouped[:, g, :],
+                )
+            for g in range(0, PASSES, 2):
+                nc.vector.quantize_mx(
+                    out=w_codes[:, g : g + 2, :].rearrange("p g n -> p (g n)").bitcast(FP8X4),
+                    scales=w_scales[:, g : g + 2, :].rearrange("p g n -> p (g n)"),
+                    in_=w_grouped[:, g : g + 2, :].rearrange("p g c -> p (g c)"),
+                )
+            return w_codes, w_scales
+
+        def multiply(w_codes, w_scales):
+            acc = acc_pool.tile([P, BATCH, BLOCK], F32, name="acc")
+            for b in range(BATCH):
+                for g in range(PASSES):
+                    nc.tensor.matmul_mx(
+                        out=acc[:, b, :],
+                        lhsT=x_codes[:, b, g, :].bitcast(FP8X4),
+                        lhsT_scale=x_scales[:, b, g, :],
+                        rhs=w_codes[:, g, :].bitcast(FP8X4),
+                        rhs_scale=w_scales[:, g, :],
+                        start=(g == 0),
+                        stop=(g == PASSES - 1),
+                    )
+            return acc
+
+        def finish(acc, dest, head, rotated):
+            result = result_pool.tile([P, BATCH, BLOCK_HEADS, HEAD_DIM], F32, name="result")
+            natural = result[:].rearrange("p b h (i t) -> p b (h i) t", t=2)
+            planes = acc[:].rearrange("p b (t j) -> p b j t", t=2)
+            if rotated:
+                nc.vector.tensor_tensor(
+                    out=natural,
+                    in0=planes,
+                    in1=cos_block[:].rearrange("p (j t) -> p j t", t=2).unsqueeze(1).to_broadcast([P, BATCH, P, 2]),
+                    op=ALU.mult,
+                )
+                by_head = acc[:].rearrange("p b (t h i) -> p b t h i", t=2, h=BLOCK_HEADS)
+                cross = result_pool.tile([P, 2, BATCH, BLOCK_HEADS, PAIRS], F32, name="cross")
+                for t in range(2):
+                    nc.vector.tensor_tensor(
+                        out=cross[:, t],
+                        in0=by_head[:, :, 1 - t, :, 0:PAIRS],
+                        in1=signed_sin[:, t, :].unsqueeze(1).unsqueeze(1).to_broadcast([P, BATCH, BLOCK_HEADS, PAIRS]),
+                        op=ALU.mult,
+                    )
+                turned = result[:, :, :, 0 : 2 * PAIRS].rearrange("p b h (i t) -> p b h i t", t=2)
+                nc.vector.tensor_tensor(
+                    out=turned, in0=turned, in1=cross[:].rearrange("p t b h i -> p b h i t"), op=ALU.add
+                )
+            else:
+                nc.vector.tensor_copy(out=natural, in_=planes)
+            for b in range(BATCH):
+                nc.sync.dma_start(
+                    out=dest[b, head : head + BLOCK_HEADS].rearrange("h p c -> p h c"), in_=result[:, b]
+                )
+
+        x_raw = consts.tile([P, BATCH, E], BF16, name="x_raw")
+        nc.sync.dma_start(out=x_raw[:], in_=hidden_states.rearrange("b p k -> p b k"))
+        w_raws = {}
+        for kb in range(PREFETCH):
+            w_raws[kb] = load_weights(kb)
+
+        position_int = consts.tile([P, 1], I32, name="position_int")
+        nc.gpsimd.iota(position_int[:], pattern=[[0, 1]], base=0, channel_multiplier=1)
+        ident = consts.tile([P, P], F32, name="ident")
+        make_identity(nc, ident[:])
+
+        position = consts.tile([P, 1], F32, name="position")
+        nc.vector.tensor_copy(out=position[:], in_=position_int[:])
+        freq = consts.tile([P, PAIRS], F32, name="freq")
+        nc.vector.memset(freq[:, 0:1], 1.0)
+        for doubling in range(5):
+            have = 2**doubling
+            nc.vector.tensor_scalar(
+                out=freq[:, have : 2 * have],
+                in0=freq[:, 0:have],
+                scalar1=ROPE_BASE ** (-have / PAIRS),
+                scalar2=None,
+                op0=ALU.mult,
+            )
+        angle = consts.tile([P, 2, PAIRS], F32, name="angle")
+        nc.vector.tensor_scalar(
+            out=angle[:, 0, :], in0=freq[:], scalar1=position[:, 0:1], scalar2=None, op0=ALU.mult
+        )
+        nc.vector.tensor_scalar(
+            out=angle[:, 1, :], in0=angle[:, 0, :], scalar1=0.5 * math.pi, scalar2=None, op0=ALU.add
+        )
+        turns = consts.tile([P, 2, PAIRS], F32, name="turns")
+        nc.vector.tensor_scalar(
+            out=turns[:], in0=angle[:], scalar1=0.5 / math.pi, scalar2=ROUND_MAGIC, op0=ALU.mult, op1=ALU.add
+        )
+        nc.vector.tensor_scalar(out=turns[:], in0=turns[:], scalar1=ROUND_MAGIC, scalar2=None, op0=ALU.subtract)
+        reduced = consts.tile([P, 2, PAIRS], F32, name="reduced")
+        nc.vector.scalar_tensor_tensor(
+            out=reduced[:], in0=turns[:], scalar=-TWO_PI_HIGH, in1=angle[:], op0=ALU.mult, op1=ALU.add
+        )
+        nc.vector.scalar_tensor_tensor(
+            out=reduced[:], in0=turns[:], scalar=-TWO_PI_LOW, in1=reduced[:], op0=ALU.mult, op1=ALU.add
+        )
+        sin_cos = consts.tile([P, 2, PAIRS], F32, name="sin_cos")
+        nc.scalar.activation(out=sin_cos[:], in_=reduced[:], func=ACT.Sin)
+        signed_sin = consts.tile([P, 2, PAIRS], F32, name="signed_sin")
+        nc.vector.tensor_scalar(
+            out=signed_sin[:, 0, :], in0=sin_cos[:, 0, :], scalar1=-1.0, scalar2=None, op0=ALU.mult
+        )
+        nc.vector.tensor_copy(out=signed_sin[:, 1, :], in_=sin_cos[:, 0, :])
+        cos_block = consts.tile([P, BLOCK], F32, name="cos_block")
+        nc.vector.memset(cos_block[:], 1.0)
+        nc.vector.tensor_copy(
+            out=cos_block[:].rearrange("p (h c) -> p h c", h=BLOCK_HEADS)[:, :, 0 : 2 * PAIRS].rearrange(
+                "p h (i t) -> p h i t", t=2
+            ),
+            in_=sin_cos[:, 1, :].unsqueeze(1).unsqueeze(3).to_broadcast([P, BLOCK_HEADS, PAIRS, 2]),
+        )
+
+        x_grouped = consts.tile([P, BATCH, PASSES, PACK * P], BF16, name="x_grouped", align_bytes=64)
+        x_codes = consts.tile([P, BATCH, PASSES, P], U32, name="x_codes", align_bytes=64)
+        x_scales = consts.tile([P, BATCH, PASSES, P], U8, name="x_scales", align_bytes=64)
+        for b in range(BATCH):
+            for g in range(0, PASSES, 2):
+                transpose_and_group(
+                    [x_raw[:, b, :].bitcast(F32)[:, (g + s) * WORDS : (g + s + 1) * WORDS] for s in range(2)],
+                    x_grouped[:, b, g : g + 2, :].rearrange("p g c -> p (g c)"),
+                )
+        for b in range(BATCH):
+            nc.vector.quantize_mx(
+                out=x_codes[:, b].rearrange("p g m -> p (g m)").bitcast(FP8X4),
+                scales=x_scales[:, b].rearrange("p g m -> p (g m)"),
+                in_=x_grouped[:, b].rearrange("p g c -> p (g c)"),
+            )
+
+        quantised = {}
+        for kb in range(BLOCKS + 1):
+            if kb + PREFETCH < BLOCKS:
+                w_raws[kb + PREFETCH] = load_weights(kb + PREFETCH)
+            if kb < BLOCKS:
+                quantised[kb] = prepare_weights(w_raws[kb])
+            if kb >= 1:
+                w_codes, w_scales = quantised[kb - 1]
+                acc = multiply(w_codes, w_scales)
+                finish(acc, blocks[kb - 1][1], blocks[kb - 1][2], blocks[kb - 1][3])

@@ -30,7 +30,8 @@ WORDS = K_PASS // 2
 BLOCK = 256
 BLOCK_HEADS = BLOCK // HEAD_DIM
 BLOCKS = 3 * SHARDS * LOCAL // BLOCK
-PREFETCH = 7
+PREFETCH = 11
+RESULTS = 12
 
 FLOPS = 2 * BATCH * P * 3 * SHARDS * LOCAL * E
 
@@ -61,7 +62,8 @@ def tile_ttcodegenattention_pa_kernel(tc, hidden_states, w_qkv, out_0, out_1, ou
         raw_pool = ctx.enter_context(tc.tile_pool(name="raw", bufs=PREFETCH + 1))
         grouped_pool = ctx.enter_context(tc.tile_pool(name="grouped", bufs=3))
         codes_pool = ctx.enter_context(tc.tile_pool(name="codes", bufs=3))
-        result_pool = ctx.enter_context(tc.tile_pool(name="result", bufs=4))
+        result_pool = ctx.enter_context(tc.tile_pool(name="result", bufs=RESULTS))
+        cross_pool = ctx.enter_context(tc.tile_pool(name="cross", bufs=2))
         bank_pool = ctx.enter_context(tc.psum_pool(name="banks", bufs=6))
         acc_pool = ctx.enter_context(tc.psum_pool(name="acc", bufs=2))
 
@@ -127,7 +129,7 @@ def tile_ttcodegenattention_pa_kernel(tc, hidden_states, w_qkv, out_0, out_1, ou
                     op=ALU.mult,
                 )
                 by_head = acc[:].rearrange("p b (t h i) -> p b t h i", t=2, h=BLOCK_HEADS)
-                cross = result_pool.tile([P, 2, BATCH, BLOCK_HEADS, PAIRS], F32, name="cross")
+                cross = cross_pool.tile([P, 2, BATCH, BLOCK_HEADS, PAIRS], F32, name="cross")
                 for t in range(2):
                     nc.vector.tensor_tensor(
                         out=cross[:, t],

@@ -30,7 +30,8 @@ WORDS = K_PASS // 2
 BLOCK = 256
 BLOCK_HEADS = BLOCK // HEAD_DIM
 BLOCKS = 3 * SHARDS * LOCAL // BLOCK
-PREFETCH = 11
+RUN = 2
+PREFETCH = 10
 RESULTS = 12
 
 FLOPS = 2 * BATCH * P * 3 * SHARDS * LOCAL * E
@@ -59,13 +60,13 @@ def tile_ttcodegenattention_pa_kernel(tc, hidden_states, w_qkv, out_0, out_1, ou
     with ExitStack() as ctx:
         ctx.enter_context(tc.manual_schedule())
         consts = ctx.enter_context(tc.tile_pool(name="consts", bufs=1))
-        raw_pool = ctx.enter_context(tc.tile_pool(name="raw", bufs=PREFETCH + 1))
-        grouped_pool = ctx.enter_context(tc.tile_pool(name="grouped", bufs=3))
-        codes_pool = ctx.enter_context(tc.tile_pool(name="codes", bufs=3))
+        raw_pool = ctx.enter_context(tc.tile_pool(name="raw", bufs=PREFETCH + RUN))
+        grouped_pool = ctx.enter_context(tc.tile_pool(name="grouped", bufs=RUN + 1))
+        codes_pool = ctx.enter_context(tc.tile_pool(name="codes", bufs=2 * RUN + 1))
         result_pool = ctx.enter_context(tc.tile_pool(name="result", bufs=RESULTS))
         cross_pool = ctx.enter_context(tc.tile_pool(name="cross", bufs=2))
-        bank_pool = ctx.enter_context(tc.psum_pool(name="banks", bufs=6))
-        acc_pool = ctx.enter_context(tc.psum_pool(name="acc", bufs=2))
+        bank_pool = ctx.enter_context(tc.psum_pool(name="banks", bufs=8 - RUN))
+        acc_pool = ctx.enter_context(tc.psum_pool(name="acc", bufs=RUN))
 
         def load_weights(kb):
             row = blocks[kb][0]
@@ -77,12 +78,12 @@ def tile_ttcodegenattention_pa_kernel(tc, hidden_states, w_qkv, out_0, out_1, ou
 
         def transpose_and_group(word_views, grouped):
             bank = bank_pool.tile([P, 2, 2, P], F32, name="bank")
-            for s in range(2):
+            for v in range(2):
                 for u in range(2):
-                    nc.tensor.transpose(bank[:, s, u, :], word_views[s][:, u * P : (u + 1) * P], ident[:])
+                    nc.tensor.transpose(bank[:, v, u, :], word_views[v][:, u * P : (u + 1) * P], ident[:])
             nc.scalar.copy(
-                out=grouped.bitcast(F32).rearrange("p (s r u) -> p s r u", s=2, u=2),
-                in_=bank[:].rearrange("p s u r -> p s r u"),
+                out=grouped.bitcast(F32).rearrange("p (v row u) -> p v row u", v=2, u=2),
+                in_=bank[:].rearrange("p v u row -> p v row u"),
             )
 
         def prepare_weights(w_raw):
@@ -103,13 +104,13 @@ def tile_ttcodegenattention_pa_kernel(tc, hidden_states, w_qkv, out_0, out_1, ou
             return w_codes, w_scales
 
         def multiply(w_codes, w_scales):
-            acc = acc_pool.tile([P, BATCH, BLOCK], F32, name="acc")
-            for b in range(BATCH):
+            acc = acc_pool.tile([P, 2, BLOCK], F32, name="acc")
+            for r in range(2):
                 for g in range(PASSES):
                     nc.tensor.matmul_mx(
-                        out=acc[:, b, :],
-                        lhsT=x_codes[:, b, g, :].bitcast(FP8X4),
-                        lhsT_scale=x_scales[:, b, g, :],
+                        out=acc[:, r, :],
+                        lhsT=x_codes[:, r, g, :].bitcast(FP8X4),
+                        lhsT_scale=x_scales[:, r, g, :],
                         rhs=w_codes[:, g, :].bitcast(FP8X4),
                         rhs_scale=w_scales[:, g, :],
                         start=(g == 0),
@@ -118,49 +119,58 @@ def tile_ttcodegenattention_pa_kernel(tc, hidden_states, w_qkv, out_0, out_1, ou
             return acc
 
         def finish(acc, dest, head, rotated):
-            result = result_pool.tile([P, BATCH, BLOCK_HEADS, HEAD_DIM], F32, name="result")
-            natural = result[:].rearrange("p b h (i t) -> p b (h i) t", t=2)
-            planes = acc[:].rearrange("p b (t j) -> p b j t", t=2)
+            result = result_pool.tile([P, BLOCK_HEADS, 2, HEAD_DIM], F32, name="result")
+            natural = result[:].rearrange("p h r (i t) -> p r h i t", t=2)
+            planes = acc[:].rearrange("p r (t h i) -> p r h i t", t=2, h=BLOCK_HEADS)
             if rotated:
                 nc.vector.tensor_tensor(
                     out=natural,
                     in0=planes,
-                    in1=cos_block[:].rearrange("p (j t) -> p j t", t=2).unsqueeze(1).to_broadcast([P, BATCH, P, 2]),
+                    in1=cos_block[:].rearrange("p r (h i t) -> p r h i t", h=BLOCK_HEADS, t=2),
                     op=ALU.mult,
                 )
-                by_head = acc[:].rearrange("p b (t h i) -> p b t h i", t=2, h=BLOCK_HEADS)
-                cross = cross_pool.tile([P, 2, BATCH, BLOCK_HEADS, PAIRS], F32, name="cross")
+                by_plane = acc[:].rearrange("p r (t h i) -> p r t h i", t=2, h=BLOCK_HEADS)
+                cross = cross_pool.tile([P, 2, BLOCK_HEADS, 2, PAIRS], F32, name="cross")
                 for t in range(2):
                     nc.vector.tensor_tensor(
-                        out=cross[:, t],
-                        in0=by_head[:, :, 1 - t, :, 0:PAIRS],
-                        in1=signed_sin[:, t, :].unsqueeze(1).unsqueeze(1).to_broadcast([P, BATCH, BLOCK_HEADS, PAIRS]),
+                        out=cross[:, t].rearrange("p h r i -> p r h i"),
+                        in0=by_plane[:, :, 1 - t, :, 0:PAIRS],
+                        in1=signed_sin[:, t].unsqueeze(2).to_broadcast([P, 2, BLOCK_HEADS, PAIRS]),
                         op=ALU.mult,
                     )
-                turned = result[:, :, :, 0 : 2 * PAIRS].rearrange("p b h (i t) -> p b h i t", t=2)
+                turned = result[:, :, :, 0 : 2 * PAIRS].rearrange("p h r (i t) -> p h r i t", t=2)
                 nc.vector.tensor_tensor(
-                    out=turned, in0=turned, in1=cross[:].rearrange("p t b h i -> p b h i t"), op=ALU.add
+                    out=turned, in0=turned, in1=cross[:].rearrange("p t h r i -> p h r i t"), op=ALU.add
                 )
             else:
                 nc.vector.tensor_copy(out=natural, in_=planes)
             for b in range(BATCH):
                 nc.sync.dma_start(
-                    out=dest[b, head : head + BLOCK_HEADS].rearrange("h p c -> p h c"), in_=result[:, b]
+                    out=dest[b, head : head + BLOCK_HEADS].rearrange("h (q r) c -> q h (r c)", r=2),
+                    in_=result[b:P:BATCH].rearrange("q h r c -> q h (r c)"),
                 )
 
-        x_raw = consts.tile([P, BATCH, E], BF16, name="x_raw")
-        nc.sync.dma_start(out=x_raw[:], in_=hidden_states.rearrange("b p k -> p b k"))
+        x_raw = consts.tile([P, 2, E], BF16, name="x_raw")
+        for b in range(BATCH):
+            nc.sync.dma_start(out=x_raw[b:P:BATCH], in_=hidden_states[b].rearrange("(q r) k -> q r k", r=2))
         w_raws = {}
         for kb in range(PREFETCH):
             w_raws[kb] = load_weights(kb)
 
-        position_int = consts.tile([P, 1], I32, name="position_int")
-        nc.gpsimd.iota(position_int[:], pattern=[[0, 1]], base=0, channel_multiplier=1)
+        partition_int = consts.tile([P, 1], I32, name="partition_int")
+        nc.gpsimd.iota(partition_int[:], pattern=[[0, 1]], base=0, channel_multiplier=1)
         ident = consts.tile([P, P], F32, name="ident")
         make_identity(nc, ident[:])
 
-        position = consts.tile([P, 1], F32, name="position")
-        nc.vector.tensor_copy(out=position[:], in_=position_int[:])
+        even_int = consts.tile([P, 1], I32, name="even_int")
+        nc.vector.tensor_scalar(
+            out=even_int[:], in0=partition_int[:], scalar1=P - 2, scalar2=None, op0=ALU.bitwise_and
+        )
+        position = consts.tile([P, 2], F32, name="position")
+        nc.vector.tensor_copy(out=position[:, 0:1], in_=even_int[:])
+        nc.vector.tensor_scalar(
+            out=position[:, 1:2], in0=position[:, 0:1], scalar1=1.0, scalar2=None, op0=ALU.add
+        )
         freq = consts.tile([P, PAIRS], F32, name="freq")
         nc.vector.memset(freq[:, 0:1], 1.0)
         for doubling in range(5):
@@ -172,64 +182,70 @@ def tile_ttcodegenattention_pa_kernel(tc, hidden_states, w_qkv, out_0, out_1, ou
                 scalar2=None,
                 op0=ALU.mult,
             )
-        angle = consts.tile([P, 2, PAIRS], F32, name="angle")
+        angle = consts.tile([P, 2, 2, PAIRS], F32, name="angle")
+        for r in range(2):
+            nc.vector.tensor_scalar(
+                out=angle[:, 0, r, :], in0=freq[:], scalar1=position[:, r : r + 1], scalar2=None, op0=ALU.mult
+            )
         nc.vector.tensor_scalar(
-            out=angle[:, 0, :], in0=freq[:], scalar1=position[:, 0:1], scalar2=None, op0=ALU.mult
+            out=angle[:, 1], in0=angle[:, 0], scalar1=0.5 * math.pi, scalar2=None, op0=ALU.add
         )
-        nc.vector.tensor_scalar(
-            out=angle[:, 1, :], in0=angle[:, 0, :], scalar1=0.5 * math.pi, scalar2=None, op0=ALU.add
-        )
-        turns = consts.tile([P, 2, PAIRS], F32, name="turns")
+        turns = consts.tile([P, 2, 2, PAIRS], F32, name="turns")
         nc.vector.tensor_scalar(
             out=turns[:], in0=angle[:], scalar1=0.5 / math.pi, scalar2=ROUND_MAGIC, op0=ALU.mult, op1=ALU.add
         )
         nc.vector.tensor_scalar(out=turns[:], in0=turns[:], scalar1=ROUND_MAGIC, scalar2=None, op0=ALU.subtract)
-        reduced = consts.tile([P, 2, PAIRS], F32, name="reduced")
+        reduced = consts.tile([P, 2, 2, PAIRS], F32, name="reduced")
         nc.vector.scalar_tensor_tensor(
             out=reduced[:], in0=turns[:], scalar=-TWO_PI_HIGH, in1=angle[:], op0=ALU.mult, op1=ALU.add
         )
         nc.vector.scalar_tensor_tensor(
             out=reduced[:], in0=turns[:], scalar=-TWO_PI_LOW, in1=reduced[:], op0=ALU.mult, op1=ALU.add
         )
-        sin_cos = consts.tile([P, 2, PAIRS], F32, name="sin_cos")
+        sin_cos = consts.tile([P, 2, 2, PAIRS], F32, name="sin_cos")
         nc.scalar.activation(out=sin_cos[:], in_=reduced[:], func=ACT.Sin)
-        signed_sin = consts.tile([P, 2, PAIRS], F32, name="signed_sin")
+        signed_sin = consts.tile([P, 2, 2, PAIRS], F32, name="signed_sin")
         nc.vector.tensor_scalar(
-            out=signed_sin[:, 0, :], in0=sin_cos[:, 0, :], scalar1=-1.0, scalar2=None, op0=ALU.mult
+            out=signed_sin[:, 0], in0=sin_cos[:, 0], scalar1=-1.0, scalar2=None, op0=ALU.mult
         )
-        nc.vector.tensor_copy(out=signed_sin[:, 1, :], in_=sin_cos[:, 0, :])
-        cos_block = consts.tile([P, BLOCK], F32, name="cos_block")
+        nc.vector.tensor_copy(out=signed_sin[:, 1], in_=sin_cos[:, 0])
+        cos_block = consts.tile([P, 2, BLOCK], F32, name="cos_block")
         nc.vector.memset(cos_block[:], 1.0)
-        nc.vector.tensor_copy(
-            out=cos_block[:].rearrange("p (h c) -> p h c", h=BLOCK_HEADS)[:, :, 0 : 2 * PAIRS].rearrange(
-                "p h (i t) -> p h i t", t=2
-            ),
-            in_=sin_cos[:, 1, :].unsqueeze(1).unsqueeze(3).to_broadcast([P, BLOCK_HEADS, PAIRS, 2]),
-        )
+        for r in range(2):
+            nc.vector.tensor_copy(
+                out=cos_block[:, r, :]
+                .rearrange("p (h c) -> p h c", h=BLOCK_HEADS)[:, :, 0 : 2 * PAIRS]
+                .rearrange("p h (i t) -> p h i t", t=2),
+                in_=sin_cos[:, 1, r, :].unsqueeze(1).unsqueeze(3).to_broadcast([P, BLOCK_HEADS, PAIRS, 2]),
+            )
 
-        x_grouped = consts.tile([P, BATCH, PASSES, PACK * P], BF16, name="x_grouped", align_bytes=64)
-        x_codes = consts.tile([P, BATCH, PASSES, P], U32, name="x_codes", align_bytes=64)
-        x_scales = consts.tile([P, BATCH, PASSES, P], U8, name="x_scales", align_bytes=64)
-        for b in range(BATCH):
+        x_grouped = consts.tile([P, 2, PASSES, PACK * P], BF16, name="x_grouped", align_bytes=64)
+        x_codes = consts.tile([P, 2, PASSES, P], U32, name="x_codes", align_bytes=64)
+        x_scales = consts.tile([P, 2, PASSES, P], U8, name="x_scales", align_bytes=64)
+        for r in range(2):
             for g in range(0, PASSES, 2):
                 transpose_and_group(
-                    [x_raw[:, b, :].bitcast(F32)[:, (g + s) * WORDS : (g + s + 1) * WORDS] for s in range(2)],
-                    x_grouped[:, b, g : g + 2, :].rearrange("p g c -> p (g c)"),
+                    [x_raw[:, r, :].bitcast(F32)[:, (g + v) * WORDS : (g + v + 1) * WORDS] for v in range(2)],
+                    x_grouped[:, r, g : g + 2, :].rearrange("p g c -> p (g c)"),
                 )
-        for b in range(BATCH):
+        for r in range(2):
             nc.vector.quantize_mx(
-                out=x_codes[:, b].rearrange("p g m -> p (g m)").bitcast(FP8X4),
-                scales=x_scales[:, b].rearrange("p g m -> p (g m)"),
-                in_=x_grouped[:, b].rearrange("p g c -> p (g c)"),
+                out=x_codes[:, r].rearrange("p g m -> p (g m)").bitcast(FP8X4),
+                scales=x_scales[:, r].rearrange("p g m -> p (g m)"),
+                in_=x_grouped[:, r].rearrange("p g c -> p (g c)"),
             )
 
         quantised = {}
-        for kb in range(BLOCKS + 1):
-            if kb + PREFETCH < BLOCKS:
-                w_raws[kb + PREFETCH] = load_weights(kb + PREFETCH)
-            if kb < BLOCKS:
+        for first in range(0, BLOCKS + RUN, RUN):
+            this_run = [kb for kb in range(first, first + RUN) if kb < BLOCKS]
+            last_run = [kb for kb in range(first - RUN, first) if kb >= 0]
+            for kb in this_run:
+                if kb + PREFETCH < BLOCKS:
+                    w_raws[kb + PREFETCH] = load_weights(kb + PREFETCH)
+            for kb in this_run:
                 quantised[kb] = prepare_weights(w_raws[kb])
-            if kb >= 1:
-                w_codes, w_scales = quantised[kb - 1]
-                acc = multiply(w_codes, w_scales)
-                finish(acc, blocks[kb - 1][1], blocks[kb - 1][2], blocks[kb - 1][3])
+            accs = {}
+            for kb in last_run:
+                accs[kb] = multiply(quantised[kb][0], quantised[kb][1])
+            for kb in last_run:
+                finish(accs[kb], blocks[kb][1], blocks[kb][2], blocks[kb][3])

import math
from contextlib import ExitStack

import concourse.mybir as mybir
from concourse.masks import make_identity

F32 = mybir.dt.float32
BF16 = mybir.dt.bfloat16
I32 = mybir.dt.int32
U32 = mybir.dt.uint32
U8 = mybir.dt.uint8
FP8X4 = mybir.dt.float8_e4m3fn_x4
ALU = mybir.AluOpType
ACT = mybir.ActivationFunctionType

P = 128
BATCH = 2
E = 2048
SHARDS = 4
LOCAL = 512
HEAD_DIM = 128
PAIRS = 32
ROPE_BASE = 10000.0

PACK = 4
K_PASS = P * PACK
PASSES = E // K_PASS
WORDS = K_PASS // 2

BLOCK = 256
BLOCK_HEADS = BLOCK // HEAD_DIM
BLOCKS = 3 * SHARDS * LOCAL // BLOCK
RUN = 2
PREFETCH = 10
RESULTS = 12

FLOPS = 2 * BATCH * P * 3 * SHARDS * LOCAL * E

ROUND_MAGIC = 12582912.0
TWO_PI_HIGH = 6.28125
TWO_PI_LOW = 2.0 * math.pi - TWO_PI_HIGH


def tile_ttcodegenattention_pa_kernel(tc, hidden_states, w_qkv, out_0, out_1, out_2):
    nc = tc.nc

    blocks = []
    for shard in range(SHARDS):
        for part_row, dest, rotated in ((0, out_0, True), (2 * LOCAL, out_1, True), (LOCAL, out_2, False)):
            for half in range(LOCAL // BLOCK):
                blocks.append(
                    (
                        shard * 3 * LOCAL + part_row + half * BLOCK,
                        dest,
                        (shard * LOCAL + half * BLOCK) // HEAD_DIM,
                        rotated,
                    )
                )

    with ExitStack() as ctx:
        ctx.enter_context(tc.manual_schedule())
        consts = ctx.enter_context(tc.tile_pool(name="consts", bufs=1))
        raw_pool = ctx.enter_context(tc.tile_pool(name="raw", bufs=PREFETCH + RUN))
        grouped_pool = ctx.enter_context(tc.tile_pool(name="grouped", bufs=RUN + 1))
        codes_pool = ctx.enter_context(tc.tile_pool(name="codes", bufs=2 * RUN + 1))
        result_pool = ctx.enter_context(tc.tile_pool(name="result", bufs=RESULTS))
        cross_pool = ctx.enter_context(tc.tile_pool(name="cross", bufs=2))
        bank_pool = ctx.enter_context(tc.psum_pool(name="banks", bufs=8 - RUN))
        acc_pool = ctx.enter_context(tc.psum_pool(name="acc", bufs=RUN))

        def load_weights(kb):
            row = blocks[kb][0]
            w_raw = raw_pool.tile([P, 2, E], BF16, name="w_raw")
            nc.sync.dma_start(
                out=w_raw[:], in_=w_qkv[row : row + BLOCK, :].rearrange("(j t) k -> j t k", t=2)
            )
            return w_raw

        def transpose_and_group(word_views, grouped):
            bank = bank_pool.tile([P, 2, 2, P], F32, name="bank")
            for v in range(2):
                for u in range(2):
                    nc.tensor.transpose(bank[:, v, u, :], word_views[v][:, u * P : (u + 1) * P], ident[:])
            nc.scalar.copy(
                out=grouped.bitcast(F32).rearrange("p (v row u) -> p v row u", v=2, u=2),
                in_=bank[:].rearrange("p v u row -> p v row u"),
            )

        def prepare_weights(w_raw):
            w_grouped = grouped_pool.tile([P, PASSES, PACK * BLOCK], BF16, name="w_grouped", align_bytes=64)
            w_codes = codes_pool.tile([P, PASSES, BLOCK], U32, name="w_codes", align_bytes=64)
            w_scales = codes_pool.tile([P, PASSES, BLOCK], U8, name="w_scales", align_bytes=64)
            for g in range(PASSES):
                transpose_and_group(
                    [w_raw[:, t, :].bitcast(F32)[:, g * WORDS : (g + 1) * WORDS] for t in range(2)],
                    w_grouped[:, g, :],
                )
            for g in range(0, PASSES, 2):
                nc.vector.quantize_mx(
                    out=w_codes[:, g : g + 2, :].rearrange("p g n -> p (g n)").bitcast(FP8X4),
                    scales=w_scales[:, g : g + 2, :].rearrange("p g n -> p (g n)"),
                    in_=w_grouped[:, g : g + 2, :].rearrange("p g c -> p (g c)"),
                )
            return w_codes, w_scales

        def multiply(w_codes, w_scales):
            acc = acc_pool.tile([P, 2, BLOCK], F32, name="acc")
            for r in range(2):
                for g in range(PASSES):
                    nc.tensor.matmul_mx(
                        out=acc[:, r, :],
                        lhsT=x_codes[:, r, g, :].bitcast(FP8X4),
                        lhsT_scale=x_scales[:, r, g, :],
                        rhs=w_codes[:, g, :].bitcast(FP8X4),
                        rhs_scale=w_scales[:, g, :],
                        start=(g == 0),
                        stop=(g == PASSES - 1),
                    )
            return acc

        def finish(acc, dest, head, rotated):
            result = result_pool.tile([P, BLOCK_HEADS, 2, HEAD_DIM], F32, name="result")
            natural = result[:].rearrange("p h r (i t) -> p r h i t", t=2)
            planes = acc[:].rearrange("p r (t h i) -> p r h i t", t=2, h=BLOCK_HEADS)
            if rotated:
                nc.vector.tensor_tensor(
                    out=natural,
                    in0=planes,
                    in1=cos_block[:].rearrange("p r (h i t) -> p r h i t", h=BLOCK_HEADS, t=2),
                    op=ALU.mult,
                )
                by_plane = acc[:].rearrange("p r (t h i) -> p r t h i", t=2, h=BLOCK_HEADS)
                cross = cross_pool.tile([P, 2, BLOCK_HEADS, 2, PAIRS], F32, name="cross")
                for t in range(2):
                    nc.vector.tensor_tensor(
                        out=cross[:, t].rearrange("p h r i -> p r h i"),
                        in0=by_plane[:, :, 1 - t, :, 0:PAIRS],
                        in1=signed_sin[:, t].unsqueeze(2).to_broadcast([P, 2, BLOCK_HEADS, PAIRS]),
                        op=ALU.mult,
                    )
                turned = result[:, :, :, 0 : 2 * PAIRS].rearrange("p h r (i t) -> p h r i t", t=2)
                nc.vector.tensor_tensor(
                    out=turned, in0=turned, in1=cross[:].rearrange("p t h r i -> p h r i t"), op=ALU.add
                )
            else:
                nc.vector.tensor_copy(out=natural, in_=planes)
            for b in range(BATCH):
                nc.sync.dma_start(
                    out=dest[b, head : head + BLOCK_HEADS].rearrange("h (q r) c -> q h (r c)", r=2),
                    in_=result[b:P:BATCH].rearrange("q h r c -> q h (r c)"),
                )

        x_raw = consts.tile([P, 2, E], BF16, name="x_raw")
        for b in range(BATCH):
            nc.sync.dma_start(out=x_raw[b:P:BATCH], in_=hidden_states[b].rearrange("(q r) k -> q r k", r=2))
        w_raws = {}
        for kb in range(PREFETCH):
            w_raws[kb] = load_weights(kb)

        partition_int = consts.tile([P, 1], I32, name="partition_int")
        nc.gpsimd.iota(partition_int[:], pattern=[[0, 1]], base=0, channel_multiplier=1)
        ident = consts.tile([P, P], F32, name="ident")
        make_identity(nc, ident[:])

        even_int = consts.tile([P, 1], I32, name="even_int")
        nc.vector.tensor_scalar(
            out=even_int[:], in0=partition_int[:], scalar1=P - 2, scalar2=None, op0=ALU.bitwise_and
        )
        position = consts.tile([P, 2], F32, name="position")
        nc.vector.tensor_copy(out=position[:, 0:1], in_=even_int[:])
        nc.vector.tensor_scalar(
            out=position[:, 1:2], in0=position[:, 0:1], scalar1=1.0, scalar2=None, op0=ALU.add
        )
        freq = consts.tile([P, PAIRS], F32, name="freq")
        nc.vector.memset(freq[:, 0:1], 1.0)
        for doubling in range(5):
            have = 2**doubling
            nc.vector.tensor_scalar(
                out=freq[:, have : 2 * have],
                in0=freq[:, 0:have],
                scalar1=ROPE_BASE ** (-have / PAIRS),
                scalar2=None,
                op0=ALU.mult,
            )
        angle = consts.tile([P, 2, 2, PAIRS], F32, name="angle")
        for r in range(2):
            nc.vector.tensor_scalar(
                out=angle[:, 0, r, :], in0=freq[:], scalar1=position[:, r : r + 1], scalar2=None, op0=ALU.mult
            )
        nc.vector.tensor_scalar(
            out=angle[:, 1], in0=angle[:, 0], scalar1=0.5 * math.pi, scalar2=None, op0=ALU.add
        )
        turns = consts.tile([P, 2, 2, PAIRS], F32, name="turns")
        nc.vector.tensor_scalar(
            out=turns[:], in0=angle[:], scalar1=0.5 / math.pi, scalar2=ROUND_MAGIC, op0=ALU.mult, op1=ALU.add
        )
        nc.vector.tensor_scalar(out=turns[:], in0=turns[:], scalar1=ROUND_MAGIC, scalar2=None, op0=ALU.subtract)
        reduced = consts.tile([P, 2, 2, PAIRS], F32, name="reduced")
        nc.vector.scalar_tensor_tensor(
            out=reduced[:], in0=turns[:], scalar=-TWO_PI_HIGH, in1=angle[:], op0=ALU.mult, op1=ALU.add
        )
        nc.vector.scalar_tensor_tensor(
            out=reduced[:], in0=turns[:], scalar=-TWO_PI_LOW, in1=reduced[:], op0=ALU.mult, op1=ALU.add
        )
        sin_cos = consts.tile([P, 2, 2, PAIRS], F32, name="sin_cos")
        nc.scalar.activation(out=sin_cos[:], in_=reduced[:], func=ACT.Sin)
        signed_sin = consts.tile([P, 2, 2, PAIRS], F32, name="signed_sin")
        nc.vector.tensor_scalar(
            out=signed_sin[:, 0], in0=sin_cos[:, 0], scalar1=-1.0, scalar2=None, op0=ALU.mult
        )
        nc.vector.tensor_copy(out=signed_sin[:, 1], in_=sin_cos[:, 0])
        cos_block = consts.tile([P, 2, BLOCK], F32, name="cos_block")
        nc.vector.memset(cos_block[:], 1.0)
        for r in range(2):
            nc.vector.tensor_copy(
                out=cos_block[:, r, :]
                .rearrange("p (h c) -> p h c", h=BLOCK_HEADS)[:, :, 0 : 2 * PAIRS]
                .rearrange("p h (i t) -> p h i t", t=2),
                in_=sin_cos[:, 1, r, :].unsqueeze(1).unsqueeze(3).to_broadcast([P, BLOCK_HEADS, PAIRS, 2]),
            )

        x_grouped = consts.tile([P, 2, PASSES, PACK * P], BF16, name="x_grouped", align_bytes=64)
        x_codes = consts.tile([P, 2, PASSES, P], U32, name="x_codes", align_bytes=64)
        x_scales = consts.tile([P, 2, PASSES, P], U8, name="x_scales", align_bytes=64)
        for r in range(2):
            for g in range(0, PASSES, 2):
                transpose_and_group(
                    [x_raw[:, r, :].bitcast(F32)[:, (g + v) * WORDS : (g + v + 1) * WORDS] for v in range(2)],
                    x_grouped[:, r, g : g + 2, :].rearrange("p g c -> p (g c)"),
                )
        for r in range(2):
            nc.vector.quantize_mx(
                out=x_codes[:, r].rearrange("p g m -> p (g m)").bitcast(FP8X4),
                scales=x_scales[:, r].rearrange("p g m -> p (g m)"),
                in_=x_grouped[:, r].rearrange("p g c -> p (g c)"),
            )

        quantised = {}
        for first in range(0, BLOCKS + RUN, RUN):
            this_run = [kb for kb in range(first, first + RUN) if kb < BLOCKS]
            last_run = [kb for kb in range(first - RUN, first) if kb >= 0]
            for kb in this_run:
                if kb + PREFETCH < BLOCKS:
                    w_raws[kb + PREFETCH] = load_weights(kb + PREFETCH)
            for kb in this_run:
                quantised[kb] = prepare_weights(w_raws[kb])
            accs = {}
            for kb in last_run:
                accs[kb] = multiply(quantised[kb][0], quantised[kb][1])
            for kb in last_run:
                finish(accs[kb], blocks[kb][1], blocks[kb][2], blocks[kb][3])
